import numpy as np
import ml_dtypes


def mxq(x, axis, fmt="e4m3"):
    dtype, down = {"e4m3": (ml_dtypes.float8_e4m3fn, 7), "e5m2": (ml_dtypes.float8_e5m2, 14)}[fmt]
    v = np.moveaxis(np.asarray(x, np.float32).astype(ml_dtypes.bfloat16).astype(np.float64), axis, -1)
    blocks = v.reshape(v.shape[:-1] + (-1, 32))
    amax = np.abs(blocks).max(-1, keepdims=True)
    byte = np.maximum(np.where(amax > 0, np.frexp(amax)[1] - 1 + 127, 0) - down, 1)
    scale = np.exp2(byte - 127.0)
    codes = (blocks / scale).astype(np.float32).astype(dtype).astype(np.float64)
    return np.moveaxis((codes * scale).reshape(v.shape), -1, axis)


WIDE = False


def mx_kscale(k):
    if not WIDE:
        return np.ones(k)
    levels = np.array([10, -10, 5, -5, 0])
    if k % 512:
        return np.exp2(np.random.permutation(np.resize(levels, k // 32))).repeat(32)
    a = np.empty((k // 512, 16))
    for p in range(k // 512):
        a[p, :8] = np.random.permutation(np.resize(levels, 8))
        for g in range(8):
            far = levels[np.abs(levels - a[p, g]) >= 10]
            a[p, g + 8] = far[np.random.randint(len(far))]
    return np.exp2(a.ravel()).repeat(32)


BF16 = ml_dtypes.bfloat16


def bf(x):
    return np.asarray(x, np.float32).astype(BF16)


def f64(x):
    return np.asarray(x).astype(np.float64)


B, R, RS, RED, F1, F2, NC = 1024, 320, 60, 16, 1024, 512, 256
C = R * RED
EPS = 1e-5
SLOPE = 0.3


def bn_train(h, gamma, beta):
    mean = h.mean(axis=0)
    var = h.var(axis=0)
    return (h - mean) * (1.0 / np.sqrt(var + EPS)) * gamma + beta


def setup_inputs():
    s = mx_kscale(C)
    sr = s.reshape(R, RED)
    sig = np.exp2(np.random.uniform(-8.0, 1.0, (R, RED)))
    off = 0.7 * np.random.standard_normal((R, RED))
    return {"h_enc": bf((np.random.standard_normal((B, R, RED)) + off) * sig),
            "enc_gamma": bf((1.0 + 0.1 * np.random.standard_normal((R, RED))) * sr),
            "enc_beta": bf(0.3 * np.random.standard_normal((R, RED)) * sr),
            "w1": bf(np.random.standard_normal((F1, C)) / np.sqrt(C) / s[None, :]),
            "b1": bf(0.3 * np.random.standard_normal(F1))}


def reference(h_enc, enc_gamma, enc_beta, w1, b1):
    h = bn_train(f64(h_enc), f64(enc_gamma), f64(enc_beta))
    h = np.where(h >= 0, h, SLOPE * h)
    c = h.reshape(B, C)
    return (mxq(c, 1, "e4m3") @ mxq(f64(w1), 1, "e4m3").T) + f64(b1)

@@ -1,0 +1,285 @@
+import concourse.mybir as mybir
+from concourse.masks import make_identity
+
+F32 = mybir.dt.float32
+BF16 = mybir.dt.bfloat16
+U32 = mybir.dt.uint32
+U8 = mybir.dt.uint8
+FP8X4 = mybir.dt.float8_e4m3fn_x4
+ALU = mybir.AluOpType
+ACT = mybir.ActivationFunctionType
+AXIS_X = mybir.AxisListType.X
+
+P = 128
+B = 1024
+C = 5120
+F = 1024
+EPS = 1e-5
+SLOPE = 0.3
+FLOPS = 2 * B * C * F
+
+K_PASS = 512
+PASSES = C // K_PASS
+PAIRS = B // (2 * P)
+ROWS = 2 * P
+BANK = 512
+V_PASSES = 8
+STEPS = PAIRS * PASSES // 2
+W_AHEAD = 4
+W_FIRST_UNIT = 28
+
+
+def tile_roibaseline_pa_kernel(tc, h_enc, enc_gamma, enc_beta, w1, b1, out):
+    nc = tc.nc
+    h2 = h_enc.rearrange("b r o -> b (r o)")
+    with tc.tile_pool(name="keep", bufs=1) as keep, \
+            tc.tile_pool(name="w_in", bufs=4) as w_in, \
+            tc.tile_pool(name="w_grouped", bufs=2) as w_grouped, \
+            tc.tile_pool(name="scalar_stats", bufs=2) as scalar_stats, \
+            tc.tile_pool(name="normed", bufs=4) as normed, \
+            tc.tile_pool(name="c_tiles", bufs=3) as c_tiles, \
+            tc.tile_pool(name="result", bufs=3) as result, \
+            tc.psum_pool(name="psum_a", bufs=4) as psum_a, \
+            tc.psum_pool(name="psum_b", bufs=4) as psum_b, \
+            tc.manual_schedule():
+        ident = keep.tile([P, P], F32, name="ident")
+        make_identity(nc, ident[:])
+        one = keep.tile([P, 1], F32, name="one")
+        nc.vector.memset(one[:], 1.0)
+        sqrt_one = keep.tile([P, 1], F32, name="sqrt_one")
+        nc.scalar.activation(out=sqrt_one[:], in_=one[:], func=ACT.Sqrt)
+
+        gb_rows = keep.tile([P, K_PASS], BF16, name="gb_rows")
+        nc.vector.memset(gb_rows[:], 0.0)
+        nc.sync.dma_start(out=gb_rows[0:PASSES, :], in_=enc_gamma.rearrange("(g x) o -> g (x o)", g=PASSES))
+        nc.sync.dma_start(out=gb_rows[32:32 + PASSES, :], in_=enc_beta.rearrange("(g x) o -> g (x o)", g=PASSES))
+        h_sb = [keep.tile([P, C], BF16, name="h_sb%d" % bt) for bt in range(2 * PAIRS)]
+        for piece in (0, 4, 1, 2, 3):
+            cols = slice(2 * K_PASS * piece, 2 * K_PASS * (piece + 1))
+            for bt in range(2):
+                nc.sync.dma_start(out=h_sb[bt][:, cols], in_=h2[bt * P:(bt + 1) * P, cols])
+        for bt in range(2, 2 * PAIRS):
+            nc.sync.dma_start(out=h_sb[bt][:], in_=h2[bt * P:(bt + 1) * P, :])
+        w_sb = {}
+
+        def load_w(g):
+            w_sb[g] = w_in.tile([P, F // P, K_PASS], BF16, name="w_sb", tag="w_sb")
+            nc.sync.dma_start(out=w_sb[g][:],
+                              in_=w1[:, g * K_PASS:(g + 1) * K_PASS].rearrange("(f p) k -> p f k", p=P))
+
+        for g in range(4):
+            load_w(g)
+
+        w_codes = keep.tile([P, PASSES, F], U32, name="w_codes", align_bytes=64)
+        w_scales = keep.tile([P, PASSES, F], U8, name="w_scales", align_bytes=64)
+        bias = keep.tile([P, F], BF16, name="bias")
+
+        gb_bank = psum_a.tile([P, BANK], F32, name="gb_bank", tag="a")
+        for u in range(2):
+            nc.tensor.transpose(out=gb_bank[:, P * u:P * (u + 1)], in_=gb_rows[:].bitcast(F32)[:, u::2],
+                                identity=ident[:])
+        gb = keep.tile([P, 64, 2, 2], F32, name="gb")
+        nc.vector.tensor_copy(out=gb[:], in_=gb_bank[:].bitcast(BF16)[:, 0:4 * P].rearrange(
+            "p (u j e) -> p j u e", u=2, e=2)[:, 0:64, :, :])
+        gb_flat = gb[:].rearrange("p j u e -> p (j u e)")
+        gamma = gb_flat[:, 0:4 * PASSES]
+        beta = gb_flat[:, 4 * 32:4 * (32 + PASSES)]
+
+        def transpose_h(bank, q, g):
+            for u in range(2):
+                for bb in range(2):
+                    words = slice(2 * P * g + u, 2 * P * (g + 1), 2)
+                    nc.tensor.transpose(out=bank[:, ROWS * u + P * bb:ROWS * u + P * bb + P],
+                                        in_=h_sb[2 * q + bb][:].bitcast(F32)[:, words],
+                                        identity=ident[:])
+
+        stats = keep.tile([P, PASSES, 2, PAIRS, 8], F32, name="stats")
+
+        def vector_unit(q, g):
+            bank = psum_b.tile([P, BANK], F32, name="v_bank", tag="b")
+            transpose_h(bank, q, g)
+            for u in range(2):
+                nc.vector.bn_stats(out=stats[:, g, u, q, 0:6],
+                                   in_=bank[:].bitcast(BF16)[:, 2 * ROWS * u:2 * ROWS * (u + 1)])
+
+        def scalar_unit(q, g):
+            bank = psum_a.tile([P, BANK], F32, name="s_bank", tag="a")
+            transpose_h(bank, q, g)
+            x = bank[:].bitcast(BF16).rearrange("p (u r e) -> p u r e", u=2, e=2)
+            sums = scalar_stats.tile([P, 4], F32, name="sums", tag="sums")
+            for u in range(2):
+                for e in range(2):
+                    unused = scalar_stats.tile([P, ROWS], BF16, name="unused", tag="unused")
+                    nc.scalar.activation(out=unused[:], in_=x[:, u, :, e], func=ACT.Identity,
+                                         accum_out=sums[:, 2 * u + e:2 * u + e + 1])
+            nc.scalar.activation(out=stats[:, g, :, q, 1:5:3], in_=sums[:].rearrange("p (u e) -> p u e", e=2),
+                                 func=ACT.Copy, scale=1.0 / ROWS)
+            for u in range(2):
+                for e in range(2):
+                    unused = scalar_stats.tile([P, ROWS], BF16, name="unused", tag="unused")
+                    nc.scalar.activation(out=unused[:], in_=x[:, u, :, e], func=ACT.Square, scale=-1.0,
+                                         bias=stats[:, g, u, q, 3 * e + 1:3 * e + 2],
+                                         accum_out=stats[:, g, u, q, 3 * e + 2:3 * e + 3])
+
+        w_bf = {}
+
+        def w_group(g):
+            w_bf[g] = w_grouped.tile([P, 4 * F], BF16, name="w_bf", tag="w_bf", align_bytes=64)
+            grouped = w_bf[g][:].bitcast(F32).rearrange("p (f u) -> p f u", u=2)
+            words = w_sb[g][:].bitcast(F32)
+            for part in range(4):
+                bank = psum_a.tile([P, BANK], F32, name="w_bank", tag="a")
+                for u in range(2):
+                    for ft in range(2):
+                        nc.tensor.transpose(out=bank[:, 2 * P * u + P * ft:2 * P * u + P * ft + P],
+                                            in_=words[:, 2 * part + ft, u::2], identity=ident[:])
+                nc.scalar.copy(out=grouped[:, 2 * P * part:2 * P * (part + 1), :],
+                               in_=bank[:].rearrange("p (u f) -> p f u", u=2))
+            if g + 4 < PASSES:
+                load_w(g + 4)
+
+        def w_quantise(g):
+            nc.vector.quantize_mx(out=w_codes[:, g, :].bitcast(FP8X4), scales=w_scales[:, g, :], in_=w_bf[g][:])
+
+        units = 0
+        for q in range(PAIRS):
+            for g in range(V_PASSES):
+                if g == 2:
+                    scalar_unit(q, V_PASSES)
+                if g == 6:
+                    scalar_unit(q, V_PASSES + 1)
+                vector_unit(q, g)
+                units += 1
+                if units >= W_FIRST_UNIT and units % 2 == 0:
+                    w_group((units - W_FIRST_UNIT) // 2)
+                    if units > W_FIRST_UNIT:
+                        w_quantise((units - W_FIRST_UNIT) // 2 - 1)
+
+        chunk_mean = stats[:, :, :, :, 1:5:3].rearrange("p g u q e -> p (g u) e q")
+        chunk_m2 = stats[:, :, :, :, 2:6:3].rearrange("p g u q e -> p (g u) e q")
+        shape3 = [P, 2 * PASSES, 2]
+        mean_sum = keep.tile(shape3, F32, name="mean_sum")
+        mean = keep.tile(shape3, F32, name="mean")
+        m2_sum = keep.tile(shape3, F32, name="m2_sum")
+        dist = keep.tile(shape3 + [PAIRS], F32, name="dist")
+        dist2 = keep.tile(shape3 + [PAIRS], F32, name="dist2")
+        dist2_sum = keep.tile(shape3, F32, name="dist2_sum")
+        flat = [P, 4 * PASSES]
+        within = keep.tile(flat, F32, name="within")
+        var_eps = keep.tile(flat, F32, name="var_eps")
+        root = keep.tile(flat, F32, name="root")
+        inv_root = keep.tile(flat, F32, name="inv_root")
+        quotient = keep.tile(flat, F32, name="quotient")
+        two_roots = keep.tile(flat, F32, name="two_roots")
+        inv_two_roots = keep.tile(flat, F32, name="inv_two_roots")
+        scale = keep.tile(flat, F32, name="scale")
+        mean_scaled = keep.tile(flat, F32, name="mean_scaled")
+        offset = keep.tile(flat, F32, name="offset")
+        nc.vector.tensor_reduce(out=mean_sum[:], in_=chunk_mean, axis=AXIS_X, op=ALU.add)
+        nc.vector.tensor_reduce(out=m2_sum[:], in_=chunk_m2, axis=AXIS_X, op=ALU.add)
+        nc.vector.tensor_scalar_mul(out=mean[:], in0=mean_sum[:], scalar1=1.0 / PAIRS)
+        nc.vector.tensor_scalar(out=within[:], in0=m2_sum[:].rearrange("p j e -> p (j e)"), scalar1=1.0 / B,
+                                scalar2=EPS, op0=ALU.mult, op1=ALU.add)
+        nc.vector.tensor_tensor(out=dist[:], in0=chunk_mean,
+                                in1=mean[:].unsqueeze(3).to_broadcast(shape3 + [PAIRS]), op=ALU.subtract)
+        nc.vector.tensor_tensor(out=dist2[:], in0=dist[:], in1=dist[:], op=ALU.mult)
+        nc.vector.tensor_reduce(out=dist2_sum[:], in_=dist2[:], axis=AXIS_X, op=ALU.add)
+        nc.vector.scalar_tensor_tensor(out=var_eps[:], in0=dist2_sum[:].rearrange("p j e -> p (j e)"),
+                                       scalar=1.0 / PAIRS, in1=within[:], op0=ALU.mult, op1=ALU.add)
+        nc.scalar.activation(out=root[:], in_=var_eps[:], func=ACT.Sqrt)
+        w_group(W_AHEAD - 1)
+        w_quantise(W_AHEAD - 2)
+
+        x_banks = {}
+        n_tiles = {}
+        c_bf = {}
+        c_mx = {}
+        acc = {}
+
+        def transposes(d):
+            for half in range(2):
+                x_banks[(d, half)] = psum_a.tile([P, BANK], F32, name="x_bank", tag="a")
+                transpose_h(x_banks[(d, half)], d // 5, 2 * (d % 5) + half)
+
+        def norm(d):
+            for half in range(2):
+                g = 2 * (d % 5) + half
+                x = x_banks[(d, half)][:].bitcast(BF16).rearrange("p (u r e) -> p u r e", u=2, e=2)
+                n_tiles[(d, half)] = normed.tile([P, 4, ROWS], F32, name="n_tile", tag="n_tile")
+                for u in range(2):
+                    for e in range(2):
+                        col = 4 * g + 2 * u + e
+                        nc.scalar.activation(out=n_tiles[(d, half)][:, 2 * u + e, :], in_=x[:, u, :, e],
+                                             func=ACT.Identity, scale=scale[:, col:col + 1],
+                                             bias=offset[:, col:col + 1])
+
+        def leaky_relu(d, half):
+            if half == 0:
+                c_bf[d] = c_tiles.tile([P, 8 * ROWS], BF16, name="c_bf", tag="c_bf", align_bytes=64)
+            n = n_tiles[(d, half)][:].rearrange("p t r -> p r t")
+            nc.vector.scalar_tensor_tensor(
+                out=c_bf[d][:, 4 * ROWS * half:4 * ROWS * (half + 1)].rearrange("p (r t) -> p r t", t=4),
+                in0=n, scalar=SLOPE, in1=n, op0=ALU.mult, op1=ALU.max)
+
+        def quantise(d):
+            codes = c_tiles.tile([P, 2 * ROWS], U32, name="c_codes", tag="c_codes", align_bytes=64)
+            scales = c_tiles.tile([P, 2 * ROWS], U8, name="c_scales", tag="c_scales", align_bytes=64)
+            c_mx[d] = (codes, scales)
+            nc.vector.quantize_mx(out=codes[:].bitcast(FP8X4), scales=scales[:], in_=c_bf[d][:])
+
+        def mx_passes(d):
+            r = d // 5
+            if d % 5 == 0:
+                acc[r] = [[psum_b.tile([P, BANK], F32, name="acc", tag="b") for fh in range(2)] for bb in range(2)]
+            codes, scales = c_mx[d]
+            for bb in range(2):
+                for fh in range(2):
+                    for half in range(2):
+                        g = 2 * (d % 5) + half
+                        rows = slice(ROWS * half + P * bb, ROWS * half + P * bb + P)
+                        outs = slice(BANK * fh, BANK * (fh + 1))
+                        nc.tensor.matmul_mx(out=acc[r][bb][fh][:],
+                                            lhsT=codes[:, rows].bitcast(FP8X4), lhsT_scale=scales[:, rows],
+                                            rhs=w_codes[:, g, outs].bitcast(FP8X4), rhs_scale=w_scales[:, g, outs],
+                                            start=(g == 0), stop=(g == PASSES - 1))
+
+        def add_bias_and_store(r):
+            for bb in range(2):
+                for fh in range(2):
+                    outs = slice(BANK * fh, BANK * (fh + 1))
+                    res = result.tile([P, BANK], F32, name="res", tag="res")
+                    nc.vector.tensor_tensor(out=res[:], in0=acc[r][bb][fh][:], in1=bias[:, outs], op=ALU.add)
+                    row0 = (2 * r + bb) * P
+                    nc.sync.dma_start(out=out[row0:row0 + P, outs], in_=res[:])
+
+        transposes(0)
+        nc.vector.reciprocal(out=inv_root[:], in_=root[:])
+        nc.vector.tensor_tensor(out=quotient[:], in0=var_eps[:], in1=inv_root[:], op=ALU.mult)
+        nc.vector.tensor_tensor(out=two_roots[:], in0=quotient[:], in1=root[:], op=ALU.add)
+        nc.vector.reciprocal(out=inv_two_roots[:], in_=two_roots[:])
+        nc.vector.scalar_tensor_tensor(out=scale[:], in0=gamma, scalar=2.0, in1=inv_two_roots[:],
+                                       op0=ALU.mult, op1=ALU.mult)
+        nc.vector.tensor_tensor(out=mean_scaled[:], in0=mean[:].rearrange("p j e -> p (j e)"), in1=scale[:],
+                                op=ALU.mult)
+        nc.vector.tensor_tensor(out=offset[:], in0=beta, in1=mean_scaled[:], op=ALU.subtract)
+        nc.sync.dma_start(out=bias[:], in_=b1.partition_broadcast(P))
+
+        for p in range(STEPS + 3):
+            if p < STEPS:
+                norm(p)
+            if p + W_AHEAD < PASSES:
+                w_group(p + W_AHEAD)
+            if p + 1 < STEPS:
+                transposes(p + 1)
+            if 1 <= p <= STEPS:
+                leaky_relu(p - 1, 0)
+            if p >= 7 and (p - 7) % 5 == 0:
+                add_bias_and_store((p - 7) // 5)
+            if 2 <= p <= STEPS + 1:
+                quantise(p - 2)
+            if 1 <= p <= STEPS:
+                leaky_relu(p - 1, 1)
+            if p + W_AHEAD - 1 < PASSES:
+                w_quantise(p + W_AHEAD - 1)
+            if 2 <= p <= STEPS + 1:
+                mx_passes(p - 2)

@@ -23,22 +23,26 @@ PASSES = C // K_PASS
 PAIRS = B // (2 * P)
 ROWS = 2 * P
 BANK = 512
-V_PASSES = 8
-STEPS = PAIRS * PASSES // 2
-W_AHEAD = 4
-W_FIRST_UNIT = 28
+KINDS = 2
+HALF = PASSES // KINDS
+STEPS = PAIRS * HALF
+MX_LAG = 3
+W_IN = 3
+FIRST = 2
+ONES = 2
 
 
 def tile_roibaseline_pa_kernel(tc, h_enc, enc_gamma, enc_beta, w1, b1, out):
     nc = tc.nc
     h2 = h_enc.rearrange("b r o -> b (r o)")
     with tc.tile_pool(name="keep", bufs=1) as keep, \
-            tc.tile_pool(name="w_in", bufs=4) as w_in, \
+            tc.tile_pool(name="w_in", bufs=W_IN) as w_in, \
             tc.tile_pool(name="w_grouped", bufs=2) as w_grouped, \
             tc.tile_pool(name="scalar_stats", bufs=2) as scalar_stats, \
-            tc.tile_pool(name="normed", bufs=4) as normed, \
+            tc.tile_pool(name="normed", bufs=3) as normed, \
             tc.tile_pool(name="c_tiles", bufs=3) as c_tiles, \
-            tc.tile_pool(name="result", bufs=3) as result, \
+            tc.tile_pool(name="c_mx_tiles", bufs=4) as c_mx_tiles, \
+            tc.tile_pool(name="result", bufs=4) as result, \
             tc.psum_pool(name="psum_a", bufs=4) as psum_a, \
             tc.psum_pool(name="psum_b", bufs=4) as psum_b, \
             tc.manual_schedule():
@@ -54,12 +58,11 @@ def tile_roibaseline_pa_kernel(tc, h_enc, enc_gamma, enc_beta, w1, b1, out):
         nc.sync.dma_start(out=gb_rows[0:PASSES, :], in_=enc_gamma.rearrange("(g x) o -> g (x o)", g=PASSES))
         nc.sync.dma_start(out=gb_rows[32:32 + PASSES, :], in_=enc_beta.rearrange("(g x) o -> g (x o)", g=PASSES))
         h_sb = [keep.tile([P, C], BF16, name="h_sb%d" % bt) for bt in range(2 * PAIRS)]
-        for piece in (0, 4, 1, 2, 3):
-            cols = slice(2 * K_PASS * piece, 2 * K_PASS * (piece + 1))
-            for bt in range(2):
-                nc.sync.dma_start(out=h_sb[bt][:, cols], in_=h2[bt * P:(bt + 1) * P, cols])
-        for bt in range(2, 2 * PAIRS):
-            nc.sync.dma_start(out=h_sb[bt][:], in_=h2[bt * P:(bt + 1) * P, :])
+        for q in range(PAIRS):
+            for i in range(HALF):
+                cols = slice(KINDS * K_PASS * i, KINDS * K_PASS * (i + 1))
+                for bt in (2 * q, 2 * q + 1):
+                    nc.sync.dma_start(out=h_sb[bt][:, cols], in_=h2[bt * P:(bt + 1) * P, cols])
         w_sb = {}
 
         def load_w(g):
@@ -67,7 +70,7 @@ def tile_roibaseline_pa_kernel(tc, h_enc, enc_gamma, enc_beta, w1, b1, out):
             nc.sync.dma_start(out=w_sb[g][:],
                               in_=w1[:, g * K_PASS:(g + 1) * K_PASS].rearrange("(f p) k -> p f k", p=P))
 
-        for g in range(4):
+        for g in range(W_IN):
             load_w(g)
 
         w_codes = keep.tile([P, PASSES, F], U32, name="w_codes", align_bytes=64)
@@ -78,12 +81,15 @@ def tile_roibaseline_pa_kernel(tc, h_enc, enc_gamma, enc_beta, w1, b1, out):
         for u in range(2):
             nc.tensor.transpose(out=gb_bank[:, P * u:P * (u + 1)], in_=gb_rows[:].bitcast(F32)[:, u::2],
                                 identity=ident[:])
-        gb = keep.tile([P, 64, 2, 2], F32, name="gb")
-        nc.vector.tensor_copy(out=gb[:], in_=gb_bank[:].bitcast(BF16)[:, 0:4 * P].rearrange(
-            "p (u j e) -> p j u e", u=2, e=2)[:, 0:64, :, :])
-        gb_flat = gb[:].rearrange("p j u e -> p (j u e)")
-        gamma = gb_flat[:, 0:4 * PASSES]
-        beta = gb_flat[:, 4 * 32:4 * (32 + PASSES)]
+        by_kind = [P, KINDS, 4 * HALF]
+        gamma = keep.tile(by_kind, F32, name="gamma")
+        beta = keep.tile(by_kind, F32, name="beta")
+        for target, row0 in ((gamma, 0), (beta, 32)):
+            for k in range(KINDS):
+                nc.vector.tensor_copy(
+                    out=target[:, k, :].rearrange("p (i u e) -> p i u e", u=2, e=2),
+                    in_=gb_bank[:].bitcast(BF16)[:, 0:4 * P].rearrange("p (u j e) -> p j u e", u=2, e=2)[
+                        :, row0 + k:row0 + PASSES:KINDS])
 
         def transpose_h(bank, q, g):
             for u in range(2):
@@ -93,33 +99,46 @@ def tile_roibaseline_pa_kernel(tc, h_enc, enc_gamma, enc_beta, w1, b1, out):
                                         in_=h_sb[2 * q + bb][:].bitcast(F32)[:, words],
                                         identity=ident[:])
 
-        stats = keep.tile([P, PASSES, 2, PAIRS, 8], F32, name="stats")
+        v_stats = keep.tile([P, HALF, 2, PAIRS, 8], F32, name="v_stats")
+        s_dist2 = keep.tile([P, HALF, 4, PAIRS], F32, name="s_dist2")
+        shift = keep.tile([P, HALF, 4], F32, name="shift")
+        sums = [keep.tile([P, HALF, 4], F32, name="sums%d" % q) for q in range(PAIRS)]
+        ones = keep.tile([P, ONES], BF16, name="ones")
+        nc.vector.memset(ones[:], 1.0)
 
-        def vector_unit(q, g):
+        def vector_unit(q, i):
             bank = psum_b.tile([P, BANK], F32, name="v_bank", tag="b")
-            transpose_h(bank, q, g)
+            transpose_h(bank, q, KINDS * i)
             for u in range(2):
-                nc.vector.bn_stats(out=stats[:, g, u, q, 0:6],
+                nc.vector.bn_stats(out=v_stats[:, i, u, q, 0:6],
                                    in_=bank[:].bitcast(BF16)[:, 2 * ROWS * u:2 * ROWS * (u + 1)])
 
-        def scalar_unit(q, g):
+        def scalar_unit(q, i):
             bank = psum_a.tile([P, BANK], F32, name="s_bank", tag="a")
-            transpose_h(bank, q, g)
+            transpose_h(bank, q, KINDS * i + 1)
             x = bank[:].bitcast(BF16).rearrange("p (u r e) -> p u r e", u=2, e=2)
-            sums = scalar_stats.tile([P, 4], F32, name="sums", tag="sums")
+            if q == 0:
+                nc.scalar.copy(out=shift[:, i, :].rearrange("p (u e) -> p u e", e=2), in_=x[:, :, 0, :])
             for u in range(2):
                 for e in range(2):
-                    unused = scalar_stats.tile([P, ROWS], BF16, name="unused", tag="unused")
-                    nc.scalar.activation(out=unused[:], in_=x[:, u, :, e], func=ACT.Identity,
-                                         accum_out=sums[:, 2 * u + e:2 * u + e + 1])
-            nc.scalar.activation(out=stats[:, g, :, q, 1:5:3], in_=sums[:].rearrange("p (u e) -> p u e", e=2),
-                                 func=ACT.Copy, scale=1.0 / ROWS)
-            for u in range(2):
-                for e in range(2):
+                    t = 2 * u + e
                     unused = scalar_stats.tile([P, ROWS], BF16, name="unused", tag="unused")
                     nc.scalar.activation(out=unused[:], in_=x[:, u, :, e], func=ACT.Square, scale=-1.0,
-                                         bias=stats[:, g, u, q, 3 * e + 1:3 * e + 2],
-                                         accum_out=stats[:, g, u, q, 3 * e + 2:3 * e + 3])
+                                         bias=shift[:, i, t:t + 1], accum_out=s_dist2[:, i, t, q:q + 1])
+
+        def tensor_sums(q, i0, i1):
+            bank = psum_b.tile([P, HALF, 4, ONES], F32, name="sum_bank", tag="b")
+            for i in range(i0, i1):
+                for t in range(4):
+                    k0 = K_PASS * (KINDS * i + 1)
+                    for bb in range(2):
+                        nc.tensor.matmul(out=bank[:, i, t, :], lhsT=h_sb[2 * q + bb][:, k0 + t:k0 + K_PASS:4],
+                                         rhs=ones[:], start=(bb == 0), stop=(bb == 1))
+            if q == 0:
+                nc.vector.tensor_copy(out=sums[0][:, i0:i1], in_=bank[:, i0:i1, :, 0])
+            else:
+                nc.vector.tensor_tensor(out=sums[q][:, i0:i1], in0=bank[:, i0:i1, :, 0], in1=sums[q - 1][:, i0:i1],
+                                        op=ALU.add)
 
         w_bf = {}
 
@@ -135,60 +154,75 @@ def tile_roibaseline_pa_kernel(tc, h_enc, enc_gamma, enc_beta, w1, b1, out):
                                             in_=words[:, 2 * part + ft, u::2], identity=ident[:])
                 nc.scalar.copy(out=grouped[:, 2 * P * part:2 * P * (part + 1), :],
                                in_=bank[:].rearrange("p (u f) -> p f u", u=2))
-            if g + 4 < PASSES:
-                load_w(g + 4)
+            if g + W_IN < PASSES:
+                load_w(g + W_IN)
 
         def w_quantise(g):
             nc.vector.quantize_mx(out=w_codes[:, g, :].bitcast(FP8X4), scales=w_scales[:, g, :], in_=w_bf[g][:])
 
-        units = 0
-        for q in range(PAIRS):
-            for g in range(V_PASSES):
-                if g == 2:
-                    scalar_unit(q, V_PASSES)
-                if g == 6:
-                    scalar_unit(q, V_PASSES + 1)
-                vector_unit(q, g)
-                units += 1
-                if units >= W_FIRST_UNIT and units % 2 == 0:
-                    w_group((units - W_FIRST_UNIT) // 2)
-                    if units > W_FIRST_UNIT:
-                        w_quantise((units - W_FIRST_UNIT) // 2 - 1)
+        def variances(i0, i1):
+            n = 4 * (i1 - i0)
+            mean = keep.tile([P, KINDS, n], F32, name="mean%d" % i0)
+            var_eps = keep.tile([P, KINDS, n], F32, name="var_eps%d" % i0)
+            mean_sum, m2_sum, dist2_sum, within, off_shift, off_shift2, s_sum, s_second = (
+                keep.tile([P, n], F32, name="%s%d" % (what, i0)) for what in (
+                    "mean_sum", "m2_sum", "dist2_sum", "within", "off_shift", "off_shift2", "s_sum", "s_second"))
+            dist = keep.tile([P, n, PAIRS], F32, name="dist%d" % i0)
+            dist2 = keep.tile([P, n, PAIRS], F32, name="dist2%d" % i0)
+            chunk_mean = v_stats[:, i0:i1, :, :, 1:5:3].rearrange("p i u q e -> p (i u) e q")
+            chunk_m2 = v_stats[:, i0:i1, :, :, 2:6:3].rearrange("p i u q e -> p (i u) e q")
+            by_e = "p (j e) -> p j e"
+            flat = "p i t -> p (i t)"
+            nc.vector.tensor_reduce(out=mean_sum[:].rearrange(by_e, e=2), in_=chunk_mean, axis=AXIS_X, op=ALU.add)
+            nc.vector.tensor_scalar_mul(out=mean[:, 1], in0=sums[PAIRS - 1][:, i0:i1].rearrange(flat), scalar1=1.0 / B)
+            nc.vector.tensor_reduce(out=m2_sum[:].rearrange(by_e, e=2), in_=chunk_m2, axis=AXIS_X, op=ALU.add)
+            nc.vector.tensor_scalar_mul(out=mean[:, 0], in0=mean_sum[:], scalar1=1.0 / PAIRS)
+            nc.vector.tensor_tensor(out=off_shift[:], in0=mean[:, 1], in1=shift[:, i0:i1].rearrange(flat),
+                                    op=ALU.subtract)
+            nc.vector.tensor_reduce(out=s_sum[:], in_=s_dist2[:, i0:i1].rearrange("p i t q -> p (i t) q"),
+                                    axis=AXIS_X, op=ALU.add)
+            nc.vector.tensor_tensor(
+                out=dist[:].rearrange("p (j e) q -> p j e q", e=2), in0=chunk_mean,
+                in1=mean[:, 0].rearrange(by_e, e=2).unsqueeze(3).to_broadcast([P, n // 2, 2, PAIRS]), op=ALU.subtract)
+            nc.vector.tensor_tensor(out=off_shift2[:], in0=off_shift[:], in1=off_shift[:], op=ALU.mult)
+            nc.vector.tensor_tensor(out=dist2[:], in0=dist[:], in1=dist[:], op=ALU.mult)
+            nc.vector.tensor_scalar(out=s_second[:], in0=s_sum[:], scalar1=1.0 / B, scalar2=EPS,
+                                    op0=ALU.mult, op1=ALU.add)
+            nc.vector.tensor_reduce(out=dist2_sum[:], in_=dist2[:], axis=AXIS_X, op=ALU.add)
+            nc.vector.tensor_scalar(out=within[:], in0=m2_sum[:], scalar1=1.0 / B, scalar2=EPS,
+                                    op0=ALU.mult, op1=ALU.add)
+            nc.vector.tensor_tensor(out=var_eps[:, 1], in0=s_second[:], in1=off_shift2[:], op=ALU.subtract)
+            nc.vector.scalar_tensor_tensor(out=var_eps[:, 0], in0=dist2_sum[:], scalar=1.0 / PAIRS,
+                                           in1=within[:], op0=ALU.mult, op1=ALU.add)
+            return mean, var_eps
 
-        chunk_mean = stats[:, :, :, :, 1:5:3].rearrange("p g u q e -> p (g u) e q")
-        chunk_m2 = stats[:, :, :, :, 2:6:3].rearrange("p g u q e -> p (g u) e q")
-        shape3 = [P, 2 * PASSES, 2]
-        mean_sum = keep.tile(shape3, F32, name="mean_sum")
-        mean = keep.tile(shape3, F32, name="mean")
-        m2_sum = keep.tile(shape3, F32, name="m2_sum")
-        dist = keep.tile(shape3 + [PAIRS], F32, name="dist")
-        dist2 = keep.tile(shape3 + [PAIRS], F32, name="dist2")
-        dist2_sum = keep.tile(shape3, F32, name="dist2_sum")
-        flat = [P, 4 * PASSES]
-        within = keep.tile(flat, F32, name="within")
-        var_eps = keep.tile(flat, F32, name="var_eps")
-        root = keep.tile(flat, F32, name="root")
-        inv_root = keep.tile(flat, F32, name="inv_root")
-        quotient = keep.tile(flat, F32, name="quotient")
-        two_roots = keep.tile(flat, F32, name="two_roots")
-        inv_two_roots = keep.tile(flat, F32, name="inv_two_roots")
-        scale = keep.tile(flat, F32, name="scale")
-        mean_scaled = keep.tile(flat, F32, name="mean_scaled")
-        offset = keep.tile(flat, F32, name="offset")
-        nc.vector.tensor_reduce(out=mean_sum[:], in_=chunk_mean, axis=AXIS_X, op=ALU.add)
-        nc.vector.tensor_reduce(out=m2_sum[:], in_=chunk_m2, axis=AXIS_X, op=ALU.add)
-        nc.vector.tensor_scalar_mul(out=mean[:], in0=mean_sum[:], scalar1=1.0 / PAIRS)
-        nc.vector.tensor_scalar(out=within[:], in0=m2_sum[:].rearrange("p j e -> p (j e)"), scalar1=1.0 / B,
-                                scalar2=EPS, op0=ALU.mult, op1=ALU.add)
-        nc.vector.tensor_tensor(out=dist[:], in0=chunk_mean,
-                                in1=mean[:].unsqueeze(3).to_broadcast(shape3 + [PAIRS]), op=ALU.subtract)
-        nc.vector.tensor_tensor(out=dist2[:], in0=dist[:], in1=dist[:], op=ALU.mult)
-        nc.vector.tensor_reduce(out=dist2_sum[:], in_=dist2[:], axis=AXIS_X, op=ALU.add)
-        nc.vector.scalar_tensor_tensor(out=var_eps[:], in0=dist2_sum[:].rearrange("p j e -> p (j e)"),
-                                       scalar=1.0 / PAIRS, in1=within[:], op0=ALU.mult, op1=ALU.add)
-        nc.scalar.activation(out=root[:], in_=var_eps[:], func=ACT.Sqrt)
-        w_group(W_AHEAD - 1)
-        w_quantise(W_AHEAD - 2)
+        def roots(i0, i1, var_eps):
+            root = keep.tile([P, KINDS, 4 * (i1 - i0)], F32, name="root%d" % i0)
+            nc.scalar.activation(out=root[:], in_=var_eps[:], func=ACT.Sqrt)
+            return root
+
+        scale_of = {}
+        offset_of = {}
+
+        def scales_and_offsets(i0, i1, mean, var_eps, root):
+            c = slice(4 * i0, 4 * i1)
+            inv_root, quotient, two_roots, inv_two_roots, scale, mean_scaled, offset = (
+                keep.tile([P, KINDS, 4 * (i1 - i0)], F32, name="%s%d" % (what, i0)) for what in (
+                    "inv_root", "quotient", "two_roots", "inv_two_roots", "scale", "mean_scaled", "offset"))
+            nc.vector.reciprocal(out=inv_root[:], in_=root[:])
+            nc.vector.tensor_tensor(out=quotient[:], in0=var_eps[:], in1=inv_root[:], op=ALU.mult)
+            nc.vector.tensor_tensor(out=two_roots[:], in0=quotient[:], in1=root[:], op=ALU.add)
+            nc.vector.reciprocal(out=inv_two_roots[:], in_=two_roots[:])
+            nc.vector.scalar_tensor_tensor(out=scale[:], in0=gamma[:, :, c], scalar=2.0, in1=inv_two_roots[:],
+                                           op0=ALU.mult, op1=ALU.mult)
+            nc.vector.tensor_tensor(out=mean_scaled[:], in0=mean[:], in1=scale[:], op=ALU.mult)
+            nc.vector.tensor_tensor(out=offset[:], in0=beta[:, :, c], in1=mean_scaled[:], op=ALU.subtract)
+            for i in range(i0, i1):
+                for k in range(KINDS):
+                    for t in range(4):
+                        col = 4 * (i - i0) + t
+                        scale_of[(KINDS * i + k, t)] = scale[:, k, col:col + 1]
+                        offset_of[(KINDS * i + k, t)] = offset[:, k, col:col + 1]
 
         x_banks = {}
         n_tiles = {}
@@ -197,46 +231,42 @@ def tile_roibaseline_pa_kernel(tc, h_enc, enc_gamma, enc_beta, w1, b1, out):
         acc = {}
 
         def transposes(d):
-            for half in range(2):
-                x_banks[(d, half)] = psum_a.tile([P, BANK], F32, name="x_bank", tag="a")
-                transpose_h(x_banks[(d, half)], d // 5, 2 * (d % 5) + half)
+            for k in range(KINDS):
+                x_banks[(d, k)] = psum_a.tile([P, BANK], F32, name="x_bank", tag="a")
+                transpose_h(x_banks[(d, k)], d // HALF, KINDS * (d % HALF) + k)
 
         def norm(d):
-            for half in range(2):
-                g = 2 * (d % 5) + half
-                x = x_banks[(d, half)][:].bitcast(BF16).rearrange("p (u r e) -> p u r e", u=2, e=2)
-                n_tiles[(d, half)] = normed.tile([P, 4, ROWS], F32, name="n_tile", tag="n_tile")
+            n_tiles[d] = normed.tile([P, 4, KINDS * ROWS], F32, name="n_tile", tag="n_tile")
+            for k in range(KINDS):
+                x = x_banks[(d, k)][:].bitcast(BF16).rearrange("p (u r e) -> p u r e", u=2, e=2)
                 for u in range(2):
                     for e in range(2):
-                        col = 4 * g + 2 * u + e
-                        nc.scalar.activation(out=n_tiles[(d, half)][:, 2 * u + e, :], in_=x[:, u, :, e],
-                                             func=ACT.Identity, scale=scale[:, col:col + 1],
-                                             bias=offset[:, col:col + 1])
+                        channel = (KINDS * (d % HALF) + k, 2 * u + e)
+                        nc.scalar.activation(out=n_tiles[d][:, 2 * u + e, ROWS * k:ROWS * (k + 1)], in_=x[:, u, :, e],
+                                             func=ACT.Identity, scale=scale_of[channel], bias=offset_of[channel])
 
-        def leaky_relu(d, half):
-            if half == 0:
-                c_bf[d] = c_tiles.tile([P, 8 * ROWS], BF16, name="c_bf", tag="c_bf", align_bytes=64)
-            n = n_tiles[(d, half)][:].rearrange("p t r -> p r t")
-            nc.vector.scalar_tensor_tensor(
-                out=c_bf[d][:, 4 * ROWS * half:4 * ROWS * (half + 1)].rearrange("p (r t) -> p r t", t=4),
-                in0=n, scalar=SLOPE, in1=n, op0=ALU.mult, op1=ALU.max)
+        def leaky_relu(d):
+            c_bf[d] = c_tiles.tile([P, 4 * KINDS * ROWS], BF16, name="c_bf", tag="c_bf", align_bytes=64)
+            n = n_tiles[d][:].rearrange("p t r -> p r t")
+            nc.vector.scalar_tensor_tensor(out=c_bf[d][:].rearrange("p (r t) -> p r t", t=4), in0=n, scalar=SLOPE,
+                                           in1=n, op0=ALU.mult, op1=ALU.max)
 
         def quantise(d):
-            codes = c_tiles.tile([P, 2 * ROWS], U32, name="c_codes", tag="c_codes", align_bytes=64)
-            scales = c_tiles.tile([P, 2 * ROWS], U8, name="c_scales", tag="c_scales", align_bytes=64)
+            codes = c_mx_tiles.tile([P, KINDS * ROWS], U32, name="c_codes", tag="c_codes", align_bytes=64)
+            scales = c_mx_tiles.tile([P, KINDS * ROWS], U8, name="c_scales", tag="c_scales", align_bytes=64)
             c_mx[d] = (codes, scales)
             nc.vector.quantize_mx(out=codes[:].bitcast(FP8X4), scales=scales[:], in_=c_bf[d][:])
 
         def mx_passes(d):
-            r = d // 5
-            if d % 5 == 0:
+            r = d // HALF
+            if d % HALF == 0:
                 acc[r] = [[psum_b.tile([P, BANK], F32, name="acc", tag="b") for fh in range(2)] for bb in range(2)]
             codes, scales = c_mx[d]
             for bb in range(2):
                 for fh in range(2):
-                    for half in range(2):
-                        g = 2 * (d % 5) + half
-                        rows = slice(ROWS * half + P * bb, ROWS * half + P * bb + P)
+                    for k in range(KINDS):
+                        g = KINDS * (d % HALF) + k
+                        rows = slice(ROWS * k + P * bb, ROWS * k + P * bb + P)
                         outs = slice(BANK * fh, BANK * (fh + 1))
                         nc.tensor.matmul_mx(out=acc[r][bb][fh][:],
                                             lhsT=codes[:, rows].bitcast(FP8X4), lhsT_scale=scales[:, rows],
@@ -252,34 +282,51 @@ def tile_roibaseline_pa_kernel(tc, h_enc, enc_gamma, enc_beta, w1, b1, out):
                     row0 = (2 * r + bb) * P
                     nc.sync.dma_start(out=out[row0:row0 + P, outs], in_=res[:])
 
+        def w_groups_of(p):
+            first = (3 * p + 1) // 2
+            return range(first, min((3 * (p + 1) + 1) // 2, PASSES)) if p >= 0 else ()
+
+        for q in range(PAIRS - 1):
+            for i in range(HALF):
+                scalar_unit(q, i)
+                vector_unit(q, i)
+            tensor_sums(q, 0, HALF)
+        for i in range(HALF):
+            scalar_unit(PAIRS - 1, i)
+            vector_unit(PAIRS - 1, i)
+            if i == FIRST - 1:
+                tensor_sums(PAIRS - 1, 0, FIRST)
+            if i == FIRST:
+                mean, var_eps = variances(0, FIRST)
+            if i == FIRST + 1:
+                root = roots(0, FIRST, var_eps)
+                scales_and_offsets(0, FIRST, mean, var_eps, root)
+        tensor_sums(PAIRS - 1, FIRST, HALF)
+        mean, var_eps = variances(FIRST, HALF)
         transposes(0)
-        nc.vector.reciprocal(out=inv_root[:], in_=root[:])
-        nc.vector.tensor_tensor(out=quotient[:], in0=var_eps[:], in1=inv_root[:], op=ALU.mult)
-        nc.vector.tensor_tensor(out=two_roots[:], in0=quotient[:], in1=root[:], op=ALU.add)
-        nc.vector.reciprocal(out=inv_two_roots[:], in_=two_roots[:])
-        nc.vector.scalar_tensor_tensor(out=scale[:], in0=gamma, scalar=2.0, in1=inv_two_roots[:],
-                                       op0=ALU.mult, op1=ALU.mult)
-        nc.vector.tensor_tensor(out=mean_scaled[:], in0=mean[:].rearrange("p j e -> p (j e)"), in1=scale[:],
-                                op=ALU.mult)
-        nc.vector.tensor_tensor(out=offset[:], in0=beta, in1=mean_scaled[:], op=ALU.subtract)
+        norm(0)
+        root = roots(FIRST, HALF, var_eps)
+        scales_and_offsets(FIRST, HALF, mean, var_eps, root)
         nc.sync.dma_start(out=bias[:], in_=b1.partition_broadcast(P))
 
+        mx_done = 0
         for p in range(STEPS + 3):
-            if p < STEPS:
+            emptied = [r for r in range(PAIRS) if HALF * (r + 1) == mx_done]
+            if p > 0 and p < STEPS:
                 norm(p)
-            if p + W_AHEAD < PASSES:
-                w_group(p + W_AHEAD)
+            for g in w_groups_of(p):
+                w_group(g)
             if p + 1 < STEPS:
                 transposes(p + 1)
+            for r in emptied:
+                add_bias_and_store(r)
             if 1 <= p <= STEPS:
-                leaky_relu(p - 1, 0)
-            if p >= 7 and (p - 7) % 5 == 0:
-                add_bias_and_store((p - 7) // 5)
+                leaky_relu(p - 1)
             if 2 <= p <= STEPS + 1:
                 quantise(p - 2)
-            if 1 <= p <= STEPS:
-                leaky_relu(p - 1, 1)
-            if p + W_AHEAD - 1 < PASSES:
-                w_quantise(p + W_AHEAD - 1)
-            if 2 <= p <= STEPS + 1:
-                mx_passes(p - 2)
+            for g in w_groups_of(p - 1):
+                w_quantise(g)
+            mx_end = p - MX_LAG + 1 if p < STEPS else min(p - 1, STEPS)
+            while mx_done < mx_end:
+                mx_passes(mx_done)
+                mx_done += 1

@@ -40,7 +40,7 @@ def tile_roibaseline_pa_kernel(tc, h_enc, enc_gamma, enc_beta, w1, b1, out):
             tc.tile_pool(name="w_grouped", bufs=2) as w_grouped, \
             tc.tile_pool(name="scalar_stats", bufs=2) as scalar_stats, \
             tc.tile_pool(name="normed", bufs=3) as normed, \
-            tc.tile_pool(name="c_tiles", bufs=3) as c_tiles, \
+            tc.tile_pool(name="c_tiles", bufs=2) as c_tiles, \
             tc.tile_pool(name="c_mx_tiles", bufs=4) as c_mx_tiles, \
             tc.tile_pool(name="result", bufs=4) as result, \
             tc.psum_pool(name="psum_a", bufs=4) as psum_a, \
@@ -58,10 +58,10 @@ def tile_roibaseline_pa_kernel(tc, h_enc, enc_gamma, enc_beta, w1, b1, out):
         nc.sync.dma_start(out=gb_rows[0:PASSES, :], in_=enc_gamma.rearrange("(g x) o -> g (x o)", g=PASSES))
         nc.sync.dma_start(out=gb_rows[32:32 + PASSES, :], in_=enc_beta.rearrange("(g x) o -> g (x o)", g=PASSES))
         h_sb = [keep.tile([P, C], BF16, name="h_sb%d" % bt) for bt in range(2 * PAIRS)]
-        for q in range(PAIRS):
+        for hf in range(2):
             for i in range(HALF):
                 cols = slice(KINDS * K_PASS * i, KINDS * K_PASS * (i + 1))
-                for bt in (2 * q, 2 * q + 1):
+                for bt in range(4 * hf, 4 * hf + 4):
                     nc.sync.dma_start(out=h_sb[bt][:, cols], in_=h2[bt * P:(bt + 1) * P, cols])
         w_sb = {}
 
@@ -100,9 +100,9 @@ def tile_roibaseline_pa_kernel(tc, h_enc, enc_gamma, enc_beta, w1, b1, out):
                                         identity=ident[:])
 
         v_stats = keep.tile([P, HALF, 2, PAIRS, 8], F32, name="v_stats")
-        s_dist2 = keep.tile([P, HALF, 4, PAIRS], F32, name="s_dist2")
+        s_dist2 = keep.tile([P, HALF, 4, 2], F32, name="s_dist2")
         shift = keep.tile([P, HALF, 4], F32, name="shift")
-        sums = [keep.tile([P, HALF, 4], F32, name="sums%d" % q) for q in range(PAIRS)]
+        sums = [keep.tile([P, HALF, 4], F32, name="sums%d" % hf) for hf in range(2)]
         ones = keep.tile([P, ONES], BF16, name="ones")
         nc.vector.memset(ones[:], 1.0)
 
@@ -113,31 +113,37 @@ def tile_roibaseline_pa_kernel(tc, h_enc, enc_gamma, enc_beta, w1, b1, out):
                 nc.vector.bn_stats(out=v_stats[:, i, u, q, 0:6],
                                    in_=bank[:].bitcast(BF16)[:, 2 * ROWS * u:2 * ROWS * (u + 1)])
 
-        def scalar_unit(q, i):
+        def scalar_unit(hf, i, u):
             bank = psum_a.tile([P, BANK], F32, name="s_bank", tag="a")
-            transpose_h(bank, q, KINDS * i + 1)
-            x = bank[:].bitcast(BF16).rearrange("p (u r e) -> p u r e", u=2, e=2)
-            if q == 0:
-                nc.scalar.copy(out=shift[:, i, :].rearrange("p (u e) -> p u e", e=2), in_=x[:, :, 0, :])
-            for u in range(2):
-                for e in range(2):
-                    t = 2 * u + e
-                    unused = scalar_stats.tile([P, ROWS], BF16, name="unused", tag="unused")
-                    nc.scalar.activation(out=unused[:], in_=x[:, u, :, e], func=ACT.Square, scale=-1.0,
-                                         bias=shift[:, i, t:t + 1], accum_out=s_dist2[:, i, t, q:q + 1])
+            g = KINDS * i + 1
+            for j in range(4):
+                nc.tensor.transpose(out=bank[:, P * j:P * (j + 1)],
+                                    in_=h_sb[4 * hf + j][:].bitcast(F32)[:, 2 * P * g + u:2 * P * (g + 1):2],
+                                    identity=ident[:])
+            x = bank[:].bitcast(BF16).rearrange("p (r e) -> p r e", e=2)
+            if hf == 0:
+                nc.scalar.copy(out=shift[:, i, 2 * u:2 * u + 2], in_=x[:, 0, :])
+            for e in range(2):
+                t = 2 * u + e
+                unused = scalar_stats.tile([P, 4 * P], BF16, name="unused", tag="unused")
+                nc.scalar.activation(out=unused[:], in_=x[:, :, e], func=ACT.Square, scale=-1.0,
+                                     bias=shift[:, i, t:t + 1], accum_out=s_dist2[:, i, t, hf:hf + 1])
 
-        def tensor_sums(q, i0, i1):
-            bank = psum_b.tile([P, HALF, 4, ONES], F32, name="sum_bank", tag="b")
-            for i in range(i0, i1):
-                for t in range(4):
-                    k0 = K_PASS * (KINDS * i + 1)
-                    for bb in range(2):
-                        nc.tensor.matmul(out=bank[:, i, t, :], lhsT=h_sb[2 * q + bb][:, k0 + t:k0 + K_PASS:4],
-                                         rhs=ones[:], start=(bb == 0), stop=(bb == 1))
-            if q == 0:
-                nc.vector.tensor_copy(out=sums[0][:, i0:i1], in_=bank[:, i0:i1, :, 0])
+        sum_banks = {}
+
+        def tensor_sums(hf, i):
+            sum_banks[(hf, i)] = psum_b.tile([P, 4, ONES], F32, name="sum_bank", tag="b")
+            for t in range(4):
+                k0 = K_PASS * (KINDS * i + 1)
+                for j in range(4):
+                    nc.tensor.matmul(out=sum_banks[(hf, i)][:, t, :], lhsT=h_sb[4 * hf + j][:, k0 + t:k0 + K_PASS:4],
+                                     rhs=ones[:], start=(j == 0), stop=(j == 3))
+
+        def keep_sums(hf, i):
+            if hf == 0:
+                nc.vector.tensor_copy(out=sums[0][:, i], in_=sum_banks[(hf, i)][:, :, 0])
             else:
-                nc.vector.tensor_tensor(out=sums[q][:, i0:i1], in0=bank[:, i0:i1, :, 0], in1=sums[q - 1][:, i0:i1],
+                nc.vector.tensor_tensor(out=sums[1][:, i], in0=sum_banks[(hf, i)][:, :, 0], in1=sums[0][:, i],
                                         op=ALU.add)
 
         w_bf = {}
@@ -174,7 +180,7 @@ def tile_roibaseline_pa_kernel(tc, h_enc, enc_gamma, enc_beta, w1, b1, out):
             by_e = "p (j e) -> p j e"
             flat = "p i t -> p (i t)"
             nc.vector.tensor_reduce(out=mean_sum[:].rearrange(by_e, e=2), in_=chunk_mean, axis=AXIS_X, op=ALU.add)
-            nc.vector.tensor_scalar_mul(out=mean[:, 1], in0=sums[PAIRS - 1][:, i0:i1].rearrange(flat), scalar1=1.0 / B)
+            nc.vector.tensor_scalar_mul(out=mean[:, 1], in0=sums[1][:, i0:i1].rearrange(flat), scalar1=1.0 / B)
             nc.vector.tensor_reduce(out=m2_sum[:].rearrange(by_e, e=2), in_=chunk_m2, axis=AXIS_X, op=ALU.add)
             nc.vector.tensor_scalar_mul(out=mean[:, 0], in0=mean_sum[:], scalar1=1.0 / PAIRS)
             nc.vector.tensor_tensor(out=off_shift[:], in0=mean[:, 1], in1=shift[:, i0:i1].rearrange(flat),
@@ -226,6 +232,7 @@ def tile_roibaseline_pa_kernel(tc, h_enc, enc_gamma, enc_beta, w1, b1, out):
 
         x_banks = {}
         n_tiles = {}
+        c_pairs = {}
         c_bf = {}
         c_mx = {}
         acc = {}
@@ -246,10 +253,17 @@ def tile_roibaseline_pa_kernel(tc, h_enc, enc_gamma, enc_beta, w1, b1, out):
                                              func=ACT.Identity, scale=scale_of[channel], bias=offset_of[channel])
 
         def leaky_relu(d):
+            c_pairs[d] = c_tiles.tile([P, 2, KINDS * ROWS, 2], BF16, name="c_pairs", tag="c_pairs")
+            for u in range(2):
+                n = n_tiles[d][:, 2 * u:2 * u + 2, :].rearrange("p e r -> p r e")
+                nc.vector.scalar_tensor_tensor(out=c_pairs[d][:, u], in0=n, scalar=SLOPE, in1=n,
+                                               op0=ALU.mult, op1=ALU.max)
+
+        def interleave(d):
             c_bf[d] = c_tiles.tile([P, 4 * KINDS * ROWS], BF16, name="c_bf", tag="c_bf", align_bytes=64)
-            n = n_tiles[d][:].rearrange("p t r -> p r t")
-            nc.vector.scalar_tensor_tensor(out=c_bf[d][:].rearrange("p (r t) -> p r t", t=4), in0=n, scalar=SLOPE,
-                                           in1=n, op0=ALU.mult, op1=ALU.max)
+            nc.vector.tensor_copy(
+                out=c_bf[d][:].bitcast(F32).rearrange("p (r u) -> p r u", u=2),
+                in_=c_pairs[d][:].rearrange("p u r e -> p (u r e)").bitcast(F32).rearrange("p (u r) -> p r u", u=2))
 
         def quantise(d):
             codes = c_mx_tiles.tile([P, KINDS * ROWS], U32, name="c_codes", tag="c_codes", align_bytes=64)
@@ -286,22 +300,24 @@ def tile_roibaseline_pa_kernel(tc, h_enc, enc_gamma, enc_beta, w1, b1, out):
             first = (3 * p + 1) // 2
             return range(first, min((3 * (p + 1) + 1) // 2, PASSES)) if p >= 0 else ()
 
-        for q in range(PAIRS - 1):
+        for hf in range(2):
             for i in range(HALF):
-                scalar_unit(q, i)
-                vector_unit(q, i)
-            tensor_sums(q, 0, HALF)
-        for i in range(HALF):
-            scalar_unit(PAIRS - 1, i)
-            vector_unit(PAIRS - 1, i)
-            if i == FIRST - 1:
-                tensor_sums(PAIRS - 1, 0, FIRST)
-            if i == FIRST:
-                mean, var_eps = variances(0, FIRST)
-            if i == FIRST + 1:
-                root = roots(0, FIRST, var_eps)
-                scales_and_offsets(0, FIRST, mean, var_eps, root)
-        tensor_sums(PAIRS - 1, FIRST, HALF)
+                vector_unit(2 * hf, i)
+                scalar_unit(hf, i, 0)
+                if hf == 1 and i == FIRST + 1:
+                    root = roots(0, FIRST, var_eps)
+                if i > 0:
+                    keep_sums(hf, i - 1)
+                elif hf == 1:
+                    keep_sums(0, HALF - 1)
+                vector_unit(2 * hf + 1, i)
+                scalar_unit(hf, i, 1)
+                tensor_sums(hf, i)
+                if hf == 1 and i == FIRST:
+                    mean, var_eps = variances(0, FIRST)
+                if hf == 1 and i == FIRST + 1:
+                    scales_and_offsets(0, FIRST, mean, var_eps, root)
+        keep_sums(1, HALF - 1)
         mean, var_eps = variances(FIRST, HALF)
         transposes(0)
         norm(0)
@@ -326,6 +342,8 @@ def tile_roibaseline_pa_kernel(tc, h_enc, enc_gamma, enc_beta, w1, b1, out):
                 quantise(p - 2)
             for g in w_groups_of(p - 1):
                 w_quantise(g)
+            if 1 <= p <= STEPS:
+                interleave(p - 1)
             mx_end = p - MX_LAG + 1 if p < STEPS else min(p - 1, STEPS)
             while mx_done < mx_end:
                 mx_passes(mx_done)

@@ -261,9 +261,12 @@ def tile_roibaseline_pa_kernel(tc, h_enc, enc_gamma, enc_beta, w1, b1, out):
 
         def interleave(d):
             c_bf[d] = c_tiles.tile([P, 4 * KINDS * ROWS], BF16, name="c_bf", tag="c_bf", align_bytes=64)
-            nc.vector.tensor_copy(
-                out=c_bf[d][:].bitcast(F32).rearrange("p (r u) -> p r u", u=2),
-                in_=c_pairs[d][:].rearrange("p u r e -> p (u r e)").bitcast(F32).rearrange("p (u r) -> p r u", u=2))
+            target = c_bf[d][:].bitcast(F32).rearrange("p (r u) -> p r u", u=2)
+            source = c_pairs[d][:].rearrange("p u r e -> p (u r e)").bitcast(F32).rearrange("p (u r) -> p r u", u=2)
+            if len(w_groups_of(d + 1)) > 0 or d == STEPS - 1:
+                nc.vector.tensor_copy(out=target, in_=source)
+            else:
+                nc.scalar.copy(out=target, in_=source)
 
         def quantise(d):
             codes = c_mx_tiles.tile([P, KINDS * ROWS], U32, name="c_codes", tag="c_codes", align_bytes=64)

import concourse.mybir as mybir
from concourse.masks import make_identity

F32 = mybir.dt.float32
BF16 = mybir.dt.bfloat16
U32 = mybir.dt.uint32
U8 = mybir.dt.uint8
FP8X4 = mybir.dt.float8_e4m3fn_x4
ALU = mybir.AluOpType
ACT = mybir.ActivationFunctionType
AXIS_X = mybir.AxisListType.X

P = 128
B = 1024
C = 5120
F = 1024
EPS = 1e-5
SLOPE = 0.3
FLOPS = 2 * B * C * F

K_PASS = 512
PASSES = C // K_PASS
PAIRS = B // (2 * P)
ROWS = 2 * P
BANK = 512
KINDS = 2
HALF = PASSES // KINDS
STEPS = PAIRS * HALF
MX_LAG = 3
W_IN = 3
FIRST = 2
ONES = 2


def tile_roibaseline_pa_kernel(tc, h_enc, enc_gamma, enc_beta, w1, b1, out):
    nc = tc.nc
    h2 = h_enc.rearrange("b r o -> b (r o)")
    with tc.tile_pool(name="keep", bufs=1) as keep, \
            tc.tile_pool(name="w_in", bufs=W_IN) as w_in, \
            tc.tile_pool(name="w_grouped", bufs=2) as w_grouped, \
            tc.tile_pool(name="scalar_stats", bufs=2) as scalar_stats, \
            tc.tile_pool(name="normed", bufs=3) as normed, \
            tc.tile_pool(name="c_tiles", bufs=2) as c_tiles, \
            tc.tile_pool(name="c_mx_tiles", bufs=4) as c_mx_tiles, \
            tc.tile_pool(name="result", bufs=4) as result, \
            tc.psum_pool(name="psum_a", bufs=4) as psum_a, \
            tc.psum_pool(name="psum_b", bufs=4) as psum_b, \
            tc.manual_schedule():
        ident = keep.tile([P, P], F32, name="ident")
        make_identity(nc, ident[:])
        one = keep.tile([P, 1], F32, name="one")
        nc.vector.memset(one[:], 1.0)
        sqrt_one = keep.tile([P, 1], F32, name="sqrt_one")
        nc.scalar.activation(out=sqrt_one[:], in_=one[:], func=ACT.Sqrt)

        gb_rows = keep.tile([P, K_PASS], BF16, name="gb_rows")
        nc.vector.memset(gb_rows[:], 0.0)
        nc.sync.dma_start(out=gb_rows[0:PASSES, :], in_=enc_gamma.rearrange("(g x) o -> g (x o)", g=PASSES))
        nc.sync.dma_start(out=gb_rows[32:32 + PASSES, :], in_=enc_beta.rearrange("(g x) o -> g (x o)", g=PASSES))
        h_sb = [keep.tile([P, C], BF16, name="h_sb%d" % bt) for bt in range(2 * PAIRS)]
        for hf in range(2):
            for i in range(HALF):
                cols = slice(KINDS * K_PASS * i, KINDS * K_PASS * (i + 1))
                for bt in range(4 * hf, 4 * hf + 4):
                    nc.sync.dma_start(out=h_sb[bt][:, cols], in_=h2[bt * P:(bt + 1) * P, cols])
        w_sb = {}

        def load_w(g):
            w_sb[g] = w_in.tile([P, F // P, K_PASS], BF16, name="w_sb", tag="w_sb")
            nc.sync.dma_start(out=w_sb[g][:],
                              in_=w1[:, g * K_PASS:(g + 1) * K_PASS].rearrange("(f p) k -> p f k", p=P))

        for g in range(W_IN):
            load_w(g)

        w_codes = keep.tile([P, PASSES, F], U32, name="w_codes", align_bytes=64)
        w_scales = keep.tile([P, PASSES, F], U8, name="w_scales", align_bytes=64)
        bias = keep.tile([P, F], BF16, name="bias")

        gb_bank = psum_a.tile([P, BANK], F32, name="gb_bank", tag="a")
        for u in range(2):
            nc.tensor.transpose(out=gb_bank[:, P * u:P * (u + 1)], in_=gb_rows[:].bitcast(F32)[:, u::2],
                                identity=ident[:])
        by_kind = [P, KINDS, 4 * HALF]
        gamma = keep.tile(by_kind, F32, name="gamma")
        beta = keep.tile(by_kind, F32, name="beta")
        for target, row0 in ((gamma, 0), (beta, 32)):
            for k in range(KINDS):
                nc.vector.tensor_copy(
                    out=target[:, k, :].rearrange("p (i u e) -> p i u e", u=2, e=2),
                    in_=gb_bank[:].bitcast(BF16)[:, 0:4 * P].rearrange("p (u j e) -> p j u e", u=2, e=2)[
                        :, row0 + k:row0 + PASSES:KINDS])

        def transpose_h(bank, q, g):
            for u in range(2):
                for bb in range(2):
                    words = slice(2 * P * g + u, 2 * P * (g + 1), 2)
                    nc.tensor.transpose(out=bank[:, ROWS * u + P * bb:ROWS * u + P * bb + P],
                                        in_=h_sb[2 * q + bb][:].bitcast(F32)[:, words],
                                        identity=ident[:])

        v_stats = keep.tile([P, HALF, 2, PAIRS, 8], F32, name="v_stats")
        s_dist2 = keep.tile([P, HALF, 4, 2], F32, name="s_dist2")
        shift = keep.tile([P, HALF, 4], F32, name="shift")
        sums = [keep.tile([P, HALF, 4], F32, name="sums%d" % hf) for hf in range(2)]
        ones = keep.tile([P, ONES], BF16, name="ones")
        nc.vector.memset(ones[:], 1.0)

        def vector_unit(q, i):
            bank = psum_b.tile([P, BANK], F32, name="v_bank", tag="b")
            transpose_h(bank, q, KINDS * i)
            for u in range(2):
                nc.vector.bn_stats(out=v_stats[:, i, u, q, 0:6],
                                   in_=bank[:].bitcast(BF16)[:, 2 * ROWS * u:2 * ROWS * (u + 1)])

        def scalar_unit(hf, i, u):
            bank = psum_a.tile([P, BANK], F32, name="s_bank", tag="a")
            g = KINDS * i + 1
            for j in range(4):
                nc.tensor.transpose(out=bank[:, P * j:P * (j + 1)],
                                    in_=h_sb[4 * hf + j][:].bitcast(F32)[:, 2 * P * g + u:2 * P * (g + 1):2],
                                    identity=ident[:])
            x = bank[:].bitcast(BF16).rearrange("p (r e) -> p r e", e=2)
            if hf == 0:
                nc.scalar.copy(out=shift[:, i, 2 * u:2 * u + 2], in_=x[:, 0, :])
            for e in range(2):
                t = 2 * u + e
                unused = scalar_stats.tile([P, 4 * P], BF16, name="unused", tag="unused")
                nc.scalar.activation(out=unused[:], in_=x[:, :, e], func=ACT.Square, scale=-1.0,
                                     bias=shift[:, i, t:t + 1], accum_out=s_dist2[:, i, t, hf:hf + 1])

        sum_banks = {}

        def tensor_sums(hf, i):
            sum_banks[(hf, i)] = psum_b.tile([P, 4, ONES], F32, name="sum_bank", tag="b")
            for t in range(4):
                k0 = K_PASS * (KINDS * i + 1)
                for j in range(4):
                    nc.tensor.matmul(out=sum_banks[(hf, i)][:, t, :], lhsT=h_sb[4 * hf + j][:, k0 + t:k0 + K_PASS:4],
                                     rhs=ones[:], start=(j == 0), stop=(j == 3))

        def keep_sums(hf, i):
            if hf == 0:
                nc.vector.tensor_copy(out=sums[0][:, i], in_=sum_banks[(hf, i)][:, :, 0])
            else:
                nc.vector.tensor_tensor(out=sums[1][:, i], in0=sum_banks[(hf, i)][:, :, 0], in1=sums[0][:, i],
                                        op=ALU.add)

        w_bf = {}

        def w_group(g):
            w_bf[g] = w_grouped.tile([P, 4 * F], BF16, name="w_bf", tag="w_bf", align_bytes=64)
            grouped = w_bf[g][:].bitcast(F32).rearrange("p (f u) -> p f u", u=2)
            words = w_sb[g][:].bitcast(F32)
            for part in range(4):
                bank = psum_a.tile([P, BANK], F32, name="w_bank", tag="a")
                for u in range(2):
                    for ft in range(2):
                        nc.tensor.transpose(out=bank[:, 2 * P * u + P * ft:2 * P * u + P * ft + P],
                                            in_=words[:, 2 * part + ft, u::2], identity=ident[:])
                nc.scalar.copy(out=grouped[:, 2 * P * part:2 * P * (part + 1), :],
                               in_=bank[:].rearrange("p (u f) -> p f u", u=2))
            if g + W_IN < PASSES:
                load_w(g + W_IN)

        def w_quantise(g):
            nc.vector.quantize_mx(out=w_codes[:, g, :].bitcast(FP8X4), scales=w_scales[:, g, :], in_=w_bf[g][:])

        def variances(i0, i1):
            n = 4 * (i1 - i0)
            mean = keep.tile([P, KINDS, n], F32, name="mean%d" % i0)
            var_eps = keep.tile([P, KINDS, n], F32, name="var_eps%d" % i0)
            mean_sum, m2_sum, dist2_sum, within, off_shift, off_shift2, s_sum, s_second = (
                keep.tile([P, n], F32, name="%s%d" % (what, i0)) for what in (
                    "mean_sum", "m2_sum", "dist2_sum", "within", "off_shift", "off_shift2", "s_sum", "s_second"))
            dist = keep.tile([P, n, PAIRS], F32, name="dist%d" % i0)
            dist2 = keep.tile([P, n, PAIRS], F32, name="dist2%d" % i0)
            chunk_mean = v_stats[:, i0:i1, :, :, 1:5:3].rearrange("p i u q e -> p (i u) e q")
            chunk_m2 = v_stats[:, i0:i1, :, :, 2:6:3].rearrange("p i u q e -> p (i u) e q")
            by_e = "p (j e) -> p j e"
            flat = "p i t -> p (i t)"
            nc.vector.tensor_reduce(out=mean_sum[:].rearrange(by_e, e=2), in_=chunk_mean, axis=AXIS_X, op=ALU.add)
            nc.vector.tensor_scalar_mul(out=mean[:, 1], in0=sums[1][:, i0:i1].rearrange(flat), scalar1=1.0 / B)
            nc.vector.tensor_reduce(out=m2_sum[:].rearrange(by_e, e=2), in_=chunk_m2, axis=AXIS_X, op=ALU.add)
            nc.vector.tensor_scalar_mul(out=mean[:, 0], in0=mean_sum[:], scalar1=1.0 / PAIRS)
            nc.vector.tensor_tensor(out=off_shift[:], in0=mean[:, 1], in1=shift[:, i0:i1].rearrange(flat),
                                    op=ALU.subtract)
            nc.vector.tensor_reduce(out=s_sum[:], in_=s_dist2[:, i0:i1].rearrange("p i t q -> p (i t) q"),
                                    axis=AXIS_X, op=ALU.add)
            nc.vector.tensor_tensor(
                out=dist[:].rearrange("p (j e) q -> p j e q", e=2), in0=chunk_mean,
                in1=mean[:, 0].rearrange(by_e, e=2).unsqueeze(3).to_broadcast([P, n // 2, 2, PAIRS]), op=ALU.subtract)
            nc.vector.tensor_tensor(out=off_shift2[:], in0=off_shift[:], in1=off_shift[:], op=ALU.mult)
            nc.vector.tensor_tensor(out=dist2[:], in0=dist[:], in1=dist[:], op=ALU.mult)
            nc.vector.tensor_scalar(out=s_second[:], in0=s_sum[:], scalar1=1.0 / B, scalar2=EPS,
                                    op0=ALU.mult, op1=ALU.add)
            nc.vector.tensor_reduce(out=dist2_sum[:], in_=dist2[:], axis=AXIS_X, op=ALU.add)
            nc.vector.tensor_scalar(out=within[:], in0=m2_sum[:], scalar1=1.0 / B, scalar2=EPS,
                                    op0=ALU.mult, op1=ALU.add)
            nc.vector.tensor_tensor(out=var_eps[:, 1], in0=s_second[:], in1=off_shift2[:], op=ALU.subtract)
            nc.vector.scalar_tensor_tensor(out=var_eps[:, 0], in0=dist2_sum[:], scalar=1.0 / PAIRS,
                                           in1=within[:], op0=ALU.mult, op1=ALU.add)
            return mean, var_eps

        def roots(i0, i1, var_eps):
            root = keep.tile([P, KINDS, 4 * (i1 - i0)], F32, name="root%d" % i0)
            nc.scalar.activation(out=root[:], in_=var_eps[:], func=ACT.Sqrt)
            return root

        scale_of = {}
        offset_of = {}

        def scales_and_offsets(i0, i1, mean, var_eps, root):
            c = slice(4 * i0, 4 * i1)
            inv_root, quotient, two_roots, inv_two_roots, scale, mean_scaled, offset = (
                keep.tile([P, KINDS, 4 * (i1 - i0)], F32, name="%s%d" % (what, i0)) for what in (
                    "inv_root", "quotient", "two_roots", "inv_two_roots", "scale", "mean_scaled", "offset"))
            nc.vector.reciprocal(out=inv_root[:], in_=root[:])
            nc.vector.tensor_tensor(out=quotient[:], in0=var_eps[:], in1=inv_root[:], op=ALU.mult)
            nc.vector.tensor_tensor(out=two_roots[:], in0=quotient[:], in1=root[:], op=ALU.add)
            nc.vector.reciprocal(out=inv_two_roots[:], in_=two_roots[:])
            nc.vector.scalar_tensor_tensor(out=scale[:], in0=gamma[:, :, c], scalar=2.0, in1=inv_two_roots[:],
                                           op0=ALU.mult, op1=ALU.mult)
            nc.vector.tensor_tensor(out=mean_scaled[:], in0=mean[:], in1=scale[:], op=ALU.mult)
            nc.vector.tensor_tensor(out=offset[:], in0=beta[:, :, c], in1=mean_scaled[:], op=ALU.subtract)
            for i in range(i0, i1):
                for k in range(KINDS):
                    for t in range(4):
                        col = 4 * (i - i0) + t
                        scale_of[(KINDS * i + k, t)] = scale[:, k, col:col + 1]
                        offset_of[(KINDS * i + k, t)] = offset[:, k, col:col + 1]

        x_banks = {}
        n_tiles = {}
        c_pairs = {}
        c_bf = {}
        c_mx = {}
        acc = {}

        def transposes(d):
            for k in range(KINDS):
                x_banks[(d, k)] = psum_a.tile([P, BANK], F32, name="x_bank", tag="a")
                transpose_h(x_banks[(d, k)], d // HALF, KINDS * (d % HALF) + k)

        def norm(d):
            n_tiles[d] = normed.tile([P, 4, KINDS * ROWS], F32, name="n_tile", tag="n_tile")
            for k in range(KINDS):
                x = x_banks[(d, k)][:].bitcast(BF16).rearrange("p (u r e) -> p u r e", u=2, e=2)
                for u in range(2):
                    for e in range(2):
                        channel = (KINDS * (d % HALF) + k, 2 * u + e)
                        nc.scalar.activation(out=n_tiles[d][:, 2 * u + e, ROWS * k:ROWS * (k + 1)], in_=x[:, u, :, e],
                                             func=ACT.Identity, scale=scale_of[channel], bias=offset_of[channel])

        def leaky_relu(d):
            c_pairs[d] = c_tiles.tile([P, 2, KINDS * ROWS, 2], BF16, name="c_pairs", tag="c_pairs")
            for u in range(2):
                n = n_tiles[d][:, 2 * u:2 * u + 2, :].rearrange("p e r -> p r e")
                nc.vector.scalar_tensor_tensor(out=c_pairs[d][:, u], in0=n, scalar=SLOPE, in1=n,
                                               op0=ALU.mult, op1=ALU.max)

        def interleave(d):
            c_bf[d] = c_tiles.tile([P, 4 * KINDS * ROWS], BF16, name="c_bf", tag="c_bf", align_bytes=64)
            target = c_bf[d][:].bitcast(F32).rearrange("p (r u) -> p r u", u=2)
            source = c_pairs[d][:].rearrange("p u r e -> p (u r e)").bitcast(F32).rearrange("p (u r) -> p r u", u=2)
            if len(w_groups_of(d + 1)) > 0 or d == STEPS - 1:
                nc.vector.tensor_copy(out=target, in_=source)
            else:
                nc.scalar.copy(out=target, in_=source)

        def quantise(d):
            codes = c_mx_tiles.tile([P, KINDS * ROWS], U32, name="c_codes", tag="c_codes", align_bytes=64)
            scales = c_mx_tiles.tile([P, KINDS * ROWS], U8, name="c_scales", tag="c_scales", align_bytes=64)
            c_mx[d] = (codes, scales)
            nc.vector.quantize_mx(out=codes[:].bitcast(FP8X4), scales=scales[:], in_=c_bf[d][:])

        def mx_passes(d):
            r = d // HALF
            if d % HALF == 0:
                acc[r] = [[psum_b.tile([P, BANK], F32, name="acc", tag="b") for fh in range(2)] for bb in range(2)]
            codes, scales = c_mx[d]
            for bb in range(2):
                for fh in range(2):
                    for k in range(KINDS):
                        g = KINDS * (d % HALF) + k
                        rows = slice(ROWS * k + P * bb, ROWS * k + P * bb + P)
                        outs = slice(BANK * fh, BANK * (fh + 1))
                        nc.tensor.matmul_mx(out=acc[r][bb][fh][:],
                                            lhsT=codes[:, rows].bitcast(FP8X4), lhsT_scale=scales[:, rows],
                                            rhs=w_codes[:, g, outs].bitcast(FP8X4), rhs_scale=w_scales[:, g, outs],
                                            start=(g == 0), stop=(g == PASSES - 1))

        def add_bias_and_store(r):
            for bb in range(2):
                for fh in range(2):
                    outs = slice(BANK * fh, BANK * (fh + 1))
                    res = result.tile([P, BANK], F32, name="res", tag="res")
                    nc.vector.tensor_tensor(out=res[:], in0=acc[r][bb][fh][:], in1=bias[:, outs], op=ALU.add)
                    row0 = (2 * r + bb) * P
                    nc.sync.dma_start(out=out[row0:row0 + P, outs], in_=res[:])

        def w_groups_of(p):
            first = (3 * p + 1) // 2
            return range(first, min((3 * (p + 1) + 1) // 2, PASSES)) if p >= 0 else ()

        for hf in range(2):
            for i in range(HALF):
                vector_unit(2 * hf, i)
                scalar_unit(hf, i, 0)
                if hf == 1 and i == FIRST + 1:
                    root = roots(0, FIRST, var_eps)
                if i > 0:
                    keep_sums(hf, i - 1)
                elif hf == 1:
                    keep_sums(0, HALF - 1)
                vector_unit(2 * hf + 1, i)
                scalar_unit(hf, i, 1)
                tensor_sums(hf, i)
                if hf == 1 and i == FIRST:
                    mean, var_eps = variances(0, FIRST)
                if hf == 1 and i == FIRST + 1:
                    scales_and_offsets(0, FIRST, mean, var_eps, root)
        keep_sums(1, HALF - 1)
        mean, var_eps = variances(FIRST, HALF)
        transposes(0)
        norm(0)
        root = roots(FIRST, HALF, var_eps)
        scales_and_offsets(FIRST, HALF, mean, var_eps, root)
        nc.sync.dma_start(out=bias[:], in_=b1.partition_broadcast(P))

        mx_done = 0
        for p in range(STEPS + 3):
            emptied = [r for r in range(PAIRS) if HALF * (r + 1) == mx_done]
            if p > 0 and p < STEPS:
                norm(p)
            for g in w_groups_of(p):
                w_group(g)
            if p + 1 < STEPS:
                transposes(p + 1)
            for r in emptied:
                add_bias_and_store(r)
            if 1 <= p <= STEPS:
                leaky_relu(p - 1)
            if 2 <= p <= STEPS + 1:
                quantise(p - 2)
            for g in w_groups_of(p - 1):
                w_quantise(g)
            if 1 <= p <= STEPS:
                interleave(p - 1)
            mx_end = p - MX_LAG + 1 if p < STEPS else min(p - 1, STEPS)
            while mx_done < mx_end:
                mx_passes(mx_done)
                mx_done += 1
